import numpy as np
import ml_dtypes


def mxq(x, axis, fmt="e4m3"):
    dtype, down = {"e4m3": (ml_dtypes.float8_e4m3fn, 7), "e5m2": (ml_dtypes.float8_e5m2, 14)}[fmt]
    v = np.moveaxis(np.asarray(x, np.float32).astype(ml_dtypes.bfloat16).astype(np.float64), axis, -1)
    blocks = v.reshape(v.shape[:-1] + (-1, 32))
    amax = np.abs(blocks).max(-1, keepdims=True)
    byte = np.maximum(np.where(amax > 0, np.frexp(amax)[1] - 1 + 127, 0) - down, 1)
    scale = np.exp2(byte - 127.0)
    codes = (blocks / scale).astype(np.float32).astype(dtype).astype(np.float64)
    return np.moveaxis((codes * scale).reshape(v.shape), -1, axis)


WIDE = False


def mx_kscale(k):
    if not WIDE:
        return np.ones(k)
    levels = np.array([10, -10, 5, -5, 0])
    a = np.random.permutation(np.resize(levels, k // 512 * 4)).reshape(k // 512, 4)
    idx = np.arange(k)
    return np.exp2(a[idx // 512, idx % 128 // 32])


BF16 = ml_dtypes.bfloat16


def bf(x):
    return np.asarray(x, np.float32).astype(BF16)


def f64(x):
    return np.asarray(x).astype(np.float64)


B, IN, HID, BLK, OUT = 4096, 512, 1024, 512, 10
NB = HID // BLK


def setup_inputs():
    s = mx_kscale(IN)
    t = np.tile(mx_kscale(BLK), NB)
    return {
        "x": bf(np.random.standard_normal((B, IN)) * s),
        "W1": bf(np.random.standard_normal((HID, IN)) / np.sqrt(IN) / s * t[:, None]),
        "b1": bf(np.random.standard_normal(HID) * 0.3 * t),
        "Wb": bf(np.random.standard_normal((NB, BLK, BLK)) * 1.4 / np.sqrt(BLK) / t.reshape(NB, 1, BLK)),
        "bb": bf(np.random.standard_normal(HID) * 0.3),
    }


def reference(x, W1, b1, Wb, bb):
    h = np.maximum((mxq(f64(x), 1, "e4m3") @ mxq(f64(W1), 1, "e4m3").T) + f64(b1), 0.0)
    hb = h.reshape(B, NB, BLK)
    yb = (mxq(hb, 2, "e4m3").transpose(1, 0, 2) @ mxq(f64(Wb), 2, "e4m3").transpose(0, 2, 1)).transpose(1, 0, 2)
    return np.maximum(yb.reshape(B, HID) + f64(bb), 0.0)

@@ -1,0 +1,235 @@
+from contextlib import ExitStack
+
+import concourse.bass as bass
+import concourse.mybir as mybir
+import concourse.tile as tile
+from concourse.masks import make_identity
+
+F32 = mybir.dt.float32
+BF16 = mybir.dt.bfloat16
+U32 = mybir.dt.uint32
+U8 = mybir.dt.uint8
+FP8X4 = mybir.dt.float8_e4m3fn_x4
+ALU = mybir.AluOpType
+ACT = mybir.ActivationFunctionType
+
+P = 128
+B, IN, HID, BLK = 4096, 512, 1024, 512
+NB = HID // BLK
+ROWS_PER_PART = B // P
+TILES = 4
+CHUNKS = ROWS_PER_PART // TILES
+CW = TILES * P
+
+FLOPS = 2 * B * HID * IN + 2 * B * HID * BLK
+
+RELU2 = ("S", "S", "S", "V")
+PINNED = False
+
+
+def tile_blockdiagmnistconvertible_pa_t_kernel(tc, x, W1, b1, Wb, bb, out):
+    nc = tc.nc
+    with ExitStack() as ctx:
+        const = ctx.enter_context(tc.tile_pool(name="const", bufs=1))
+        xin = ctx.enter_context(tc.tile_pool(name="xin", bufs=1))
+        win = ctx.enter_context(tc.tile_pool(name="win", bufs=1))
+        wq = ctx.enter_context(tc.tile_pool(name="wq", bufs=1))
+        wgp = ctx.enter_context(tc.tile_pool(name="wgp", bufs=2))
+        xq = ctx.enter_context(tc.tile_pool(name="xq", bufs=3))
+        hp = ctx.enter_context(tc.tile_pool(name="hp", bufs=3))
+        zp = ctx.enter_context(tc.tile_pool(name="zp", bufs=3))
+        ps_tr = ctx.enter_context(tc.psum_pool(name="ps_tr", bufs=2))
+        ps_s1 = ctx.enter_context(tc.psum_pool(name="ps_s1", bufs=3))
+        ps_s2 = ctx.enter_context(tc.psum_pool(name="ps_s2", bufs=3))
+        if PINNED:
+            ctx.enter_context(tc.manual_schedule())
+
+        x_v = x.rearrange("(p i) k -> p (i k)", i=ROWS_PER_PART)
+        out_v = out.rearrange("(p i) o -> p (i o)", i=ROWS_PER_PART)
+
+        xs = []
+        for c in range(CHUNKS):
+            xs.append(xin.tile([P, TILES * IN], BF16, name="xs%d" % c))
+        w1s = [win.tile([P, 4 * IN], BF16, name="w1s%d" % n) for n in range(NB)]
+        wbs = [win.tile([P, 4 * BLK], BF16, name="wbs%d" % n) for n in range(NB)]
+
+        def load_x(c):
+            nc.sync.dma_start(out=xs[c][:], in_=x_v[:, c * TILES * IN : (c + 1) * TILES * IN])
+
+        def load_w1(n):
+            nc.sync.dma_start(
+                out=w1s[n][:],
+                in_=W1[n * BLK : (n + 1) * BLK, :].rearrange("(p t) k -> p (t k)", t=4),
+            )
+
+        def load_wb(n):
+            nc.sync.dma_start(
+                out=wbs[n][:].rearrange("p (j k) -> p j k", j=4),
+                in_=Wb[n].rearrange("(j p) k -> p j k", p=P),
+            )
+
+        b1b = const.tile([P, 2 * 4], BF16, name="b1b")
+        bbb = const.tile([P, HID], BF16, name="bbb")
+        nc.scalar.dma_start(
+            out=b1b[:].rearrange("p (n t) -> p n t", t=4),
+            in_=b1.rearrange("(n p t) -> p n t", n=NB, t=4),
+        )
+        load_x(0)
+        load_w1(0)
+        load_w1(1)
+        load_x(1)
+        load_wb(0)
+        load_wb(1)
+        nc.scalar.dma_start(out=bbb[:], in_=bb.partition_broadcast(P))
+        for c in range(2, CHUNKS):
+            load_x(c)
+
+        ident = const.tile([P, P], F32, name="ident")
+        make_identity(nc, ident[:])
+        b1f = const.tile([P, 2 * 4], F32, name="b1f")
+        nc.vector.tensor_copy(out=b1f[:], in_=b1b[:])
+
+        def copy_words(eng, dst, src):
+            if eng == "S":
+                nc.scalar.copy(out=dst, in_=src)
+            else:
+                nc.vector.tensor_copy(out=dst, in_=src)
+
+        def transpose_group(src_words, grouped, engines):
+            g32 = grouped[:].bitcast(F32).rearrange("p (c u) -> p c u", u=2)
+            for h in range(2):
+                pt = ps_tr.tile([P, 512], F32, name="pt")
+                for il in range(2):
+                    for u in range(2):
+                        nc.tensor.transpose(
+                            pt[:, u * 256 + il * P : u * 256 + (il + 1) * P],
+                            src_words(2 * h + il, u),
+                            ident[:],
+                        )
+                copy_words(
+                    engines[h],
+                    g32[:, h * 256 : (h + 1) * 256, :],
+                    pt[:].rearrange("p (u c) -> p c u", u=2),
+                )
+
+        def quantise(grouped, codes, scales):
+            nc.vector.quantize_mx(out=codes[:].bitcast(FP8X4), scales=scales[:], in_=grouped[:])
+
+        w1c = [wq.tile([P, 512], U32, name="w1c%d" % n, align_bytes=64) for n in range(NB)]
+        w1sc = [wq.tile([P, 512], U8, name="w1sc%d" % n, align_bytes=64) for n in range(NB)]
+        wbc = [wq.tile([P, 512], U32, name="wbc%d" % n, align_bytes=64) for n in range(NB)]
+        wbsc = [wq.tile([P, 512], U8, name="wbsc%d" % n, align_bytes=64) for n in range(NB)]
+
+        def prep_w1(n):
+            w32 = w1s[n][:].bitcast(F32)
+            wg = wgp.tile([P, 2048], BF16, name="wg", align_bytes=64)
+            transpose_group(
+                lambda t, u: w32[:, t * 256 + u * P : t * 256 + (u + 1) * P], wg, ("V", "S")
+            )
+            quantise(wg, w1c[n], w1sc[n])
+
+        def prep_wb(n):
+            w32 = wbs[n][:].bitcast(F32).rearrange("p (j q u) -> p j q u", j=4, u=2)
+            wg = wgp.tile([P, 2048], BF16, name="wg", align_bytes=64)
+            transpose_group(lambda j, u: w32[:, j, :, u], wg, ("V", "S"))
+            quantise(wg, wbc[n], wbsc[n])
+
+        xcs = {}
+
+        def xpath(c):
+            x32 = xs[c][:].bitcast(F32)
+            xg = xq.tile([P, 2048], BF16, name="xg", align_bytes=64)
+            transpose_group(
+                lambda i, u: x32[:, i * 256 + u * P : i * 256 + (u + 1) * P], xg, ("S", "S")
+            )
+            xc = xq.tile([P, CW], U32, name="xc", align_bytes=64)
+            xsc = xq.tile([P, CW], U8, name="xsc", align_bytes=64)
+            quantise(xg, xc, xsc)
+            xcs[c] = (xc, xsc)
+
+        hcs = {}
+
+        def stage1(c):
+            xc, xsc = xcs[c]
+            for n in range(NB):
+                hT = hp.tile([P, 4 * CW], BF16, name="hT")
+                for t in range(4):
+                    acc = ps_s1.tile([P, CW], F32, name="acc1")
+                    nc.tensor.matmul_mx(
+                        out=acc[:],
+                        lhsT=w1c[n][:, t * P : (t + 1) * P].bitcast(FP8X4),
+                        lhsT_scale=w1sc[n][:, t * P : (t + 1) * P],
+                        rhs=xc[:].bitcast(FP8X4),
+                        rhs_scale=xsc[:],
+                        start=True,
+                        stop=True,
+                    )
+                    nc.scalar.activation(
+                        out=hT[:, t * CW : (t + 1) * CW],
+                        in_=acc[:],
+                        func=ACT.Relu,
+                        bias=b1f[:, 4 * n + t : 4 * n + t + 1],
+                        scale=1.0,
+                    )
+                hg = hp.tile([P, 4 * CW], BF16, name="hg", align_bytes=64)
+                nc.vector.tensor_copy(
+                    out=hg[:].rearrange("p (c i t) -> p c t i", i=4, t=4),
+                    in_=hT[:].rearrange("p (t c i) -> p c t i", t=4, i=4),
+                )
+                hc = hp.tile([P, CW], U32, name="hc%d" % n, align_bytes=64)
+                hsc = hp.tile([P, CW], U8, name="hsc%d" % n, align_bytes=64)
+                quantise(hg, hc, hsc)
+                hcs[(c, n)] = (hc, hsc)
+
+        def relu2(eng, ap):
+            if eng == "V":
+                nc.vector.tensor_scalar_max(out=ap, in0=ap, scalar1=0.0)
+            elif eng == "S":
+                nc.scalar.activation(out=ap, in_=ap, func=ACT.Relu)
+            else:
+                nc.gpsimd.tensor_scalar(
+                    out=ap, in0=ap, scalar1=0.0, scalar2=0.0, op0=ALU.max, op1=ALU.add
+                )
+
+        def stage2(c):
+            z = zp.tile([P, TILES * HID], F32, name="z")
+            for il in range(TILES):
+                for n in range(NB):
+                    hc, hsc = hcs[(c, n)]
+                    acc = ps_s2.tile([P, BLK], F32, name="acc2")
+                    nc.tensor.matmul_mx(
+                        out=acc[:],
+                        lhsT=hc[:, il * P : (il + 1) * P].bitcast(FP8X4),
+                        lhsT_scale=hsc[:, il * P : (il + 1) * P],
+                        rhs=wbc[n][:].bitcast(FP8X4),
+                        rhs_scale=wbsc[n][:],
+                        start=True,
+                        stop=True,
+                    )
+                    nc.vector.tensor_tensor(
+                        out=z[:, il * HID + n * BLK : il * HID + (n + 1) * BLK],
+                        in0=acc[:],
+                        in1=bbb[:, n * BLK : (n + 1) * BLK],
+                        op=ALU.add,
+                    )
+                relu2(RELU2[il], z[:, il * HID : (il + 1) * HID])
+                if il % 2 == 1:
+                    lo = (il - 1) * HID
+                    hi = (il + 1) * HID
+                    nc.sync.dma_start(
+                        out=out_v[:, c * TILES * HID + lo : c * TILES * HID + hi], in_=z[:, lo:hi]
+                    )
+
+        xpath(0)
+        prep_w1(0)
+        prep_w1(1)
+        xpath(1)
+        stage1(0)
+        prep_wb(0)
+        prep_wb(1)
+        for c in range(1, CHUNKS):
+            if c + 1 < CHUNKS:
+                xpath(c + 1)
+            stage1(c)
+            stage2(c - 1)
+        stage2(CHUNKS - 1)

@@ -23,7 +23,8 @@ CW = TILES * P
 
 FLOPS = 2 * B * HID * IN + 2 * B * HID * BLK
 
-RELU2 = ("S", "S", "S", "V")
+RELU2 = ("G", "G", "G", "G")
+REGROUP = ("V", "S")
 PINNED = False
 
 
@@ -142,8 +143,8 @@ def tile_blockdiagmnistconvertible_pa_t_kernel(tc, x, W1, b1, Wb, bb, out):
             transpose_group(
                 lambda i, u: x32[:, i * 256 + u * P : i * 256 + (u + 1) * P], xg, ("S", "S")
             )
-            xc = xq.tile([P, CW], U32, name="xc", align_bytes=64)
-            xsc = xq.tile([P, CW], U8, name="xsc", align_bytes=64)
+            xc = xq.tile([P, CW], U32, name="xc", align_bytes=64, bufs=4)
+            xsc = xq.tile([P, CW], U8, name="xsc", align_bytes=64, bufs=4)
             quantise(xg, xc, xsc)
             xcs[c] = (xc, xsc)
 
@@ -172,9 +173,10 @@ def tile_blockdiagmnistconvertible_pa_t_kernel(tc, x, W1, b1, Wb, bb, out):
                         scale=1.0,
                     )
                 hg = hp.tile([P, 4 * CW], BF16, name="hg", align_bytes=64)
-                nc.vector.tensor_copy(
-                    out=hg[:].rearrange("p (c i t) -> p c t i", i=4, t=4),
-                    in_=hT[:].rearrange("p (t c i) -> p c t i", t=4, i=4),
+                copy_words(
+                    REGROUP[n],
+                    hg[:].rearrange("p (c i t) -> p c t i", i=4, t=4),
+                    hT[:].rearrange("p (t c i) -> p c t i", t=4, i=4),
                 )
                 hc = hp.tile([P, CW], U32, name="hc%d" % n, align_bytes=64)
                 hsc = hp.tile([P, CW], U8, name="hsc%d" % n, align_bytes=64)

@@ -26,6 +26,7 @@ FLOPS = 2 * B * HID * IN + 2 * B * HID * BLK
 RELU2 = ("G", "G", "G", "G")
 REGROUP = ("V", "S")
 PINNED = False
+FLT_MAX = 3.4028234663852886e38
 
 
 def tile_blockdiagmnistconvertible_pa_t_kernel(tc, x, W1, b1, Wb, bb, out):
@@ -190,7 +191,7 @@ def tile_blockdiagmnistconvertible_pa_t_kernel(tc, x, W1, b1, Wb, bb, out):
                 nc.scalar.activation(out=ap, in_=ap, func=ACT.Relu)
             else:
                 nc.gpsimd.tensor_scalar(
-                    out=ap, in0=ap, scalar1=0.0, scalar2=0.0, op0=ALU.max, op1=ALU.add
+                    out=ap, in0=ap, scalar1=FLT_MAX, scalar2=0.0, op0=ALU.min, op1=ALU.max
                 )
 
         def stage2(c):

@@ -1,8 +1,6 @@
 from contextlib import ExitStack
 
-import concourse.bass as bass
 import concourse.mybir as mybir
-import concourse.tile as tile
 from concourse.masks import make_identity
 
 F32 = mybir.dt.float32
@@ -23,10 +21,9 @@ CW = TILES * P
 
 FLOPS = 2 * B * HID * IN + 2 * B * HID * BLK
 
-RELU2 = ("G", "G", "G", "G")
-REGROUP = ("V", "S")
-PINNED = False
-FLT_MAX = 3.4028234663852886e38
+
+def relu2_engines(c):
+    return ("S", "S", "S", "V")
 
 
 def tile_blockdiagmnistconvertible_pa_t_kernel(tc, x, W1, b1, Wb, bb, out):
@@ -37,21 +34,17 @@ def tile_blockdiagmnistconvertible_pa_t_kernel(tc, x, W1, b1, Wb, bb, out):
         win = ctx.enter_context(tc.tile_pool(name="win", bufs=1))
         wq = ctx.enter_context(tc.tile_pool(name="wq", bufs=1))
         wgp = ctx.enter_context(tc.tile_pool(name="wgp", bufs=2))
-        xq = ctx.enter_context(tc.tile_pool(name="xq", bufs=3))
+        xq = ctx.enter_context(tc.tile_pool(name="xq", bufs=4))
         hp = ctx.enter_context(tc.tile_pool(name="hp", bufs=3))
         zp = ctx.enter_context(tc.tile_pool(name="zp", bufs=3))
         ps_tr = ctx.enter_context(tc.psum_pool(name="ps_tr", bufs=2))
         ps_s1 = ctx.enter_context(tc.psum_pool(name="ps_s1", bufs=3))
         ps_s2 = ctx.enter_context(tc.psum_pool(name="ps_s2", bufs=3))
-        if PINNED:
-            ctx.enter_context(tc.manual_schedule())
 
         x_v = x.rearrange("(p i) k -> p (i k)", i=ROWS_PER_PART)
         out_v = out.rearrange("(p i) o -> p (i o)", i=ROWS_PER_PART)
 
-        xs = []
-        for c in range(CHUNKS):
-            xs.append(xin.tile([P, TILES * IN], BF16, name="xs%d" % c))
+        xs = [xin.tile([P, TILES * IN], BF16, name="xs%d" % c) for c in range(CHUNKS)]
         w1s = [win.tile([P, 4 * IN], BF16, name="w1s%d" % n) for n in range(NB)]
         wbs = [win.tile([P, 4 * BLK], BF16, name="wbs%d" % n) for n in range(NB)]
 
@@ -71,7 +64,11 @@ def tile_blockdiagmnistconvertible_pa_t_kernel(tc, x, W1, b1, Wb, bb, out):
             )
 
         b1b = const.tile([P, 2 * 4], BF16, name="b1b")
-        bbb = const.tile([P, HID], BF16, name="bbb")
+        bbrow = const.tile([P, HID], BF16, name="bbrow")
+        ones = const.tile([P, P], BF16, name="ones")
+        nc.vector.memset(bbrow[:], 0.0)
+        nc.vector.memset(ones[:], 1.0)
+        nc.scalar.dma_start(out=bbrow[0:1, :], in_=bb.rearrange("(o n) -> o n", o=1))
         nc.scalar.dma_start(
             out=b1b[:].rearrange("p (n t) -> p n t", t=4),
             in_=b1.rearrange("(n p t) -> p n t", n=NB, t=4),
@@ -82,7 +79,6 @@ def tile_blockdiagmnistconvertible_pa_t_kernel(tc, x, W1, b1, Wb, bb, out):
         load_x(1)
         load_wb(0)
         load_wb(1)
-        nc.scalar.dma_start(out=bbb[:], in_=bb.partition_broadcast(P))
         for c in range(2, CHUNKS):
             load_x(c)
 
@@ -91,7 +87,15 @@ def tile_blockdiagmnistconvertible_pa_t_kernel(tc, x, W1, b1, Wb, bb, out):
         b1f = const.tile([P, 2 * 4], F32, name="b1f")
         nc.vector.tensor_copy(out=b1f[:], in_=b1b[:])
 
-        def copy_words(eng, dst, src):
+        bbb = const.tile([P, HID], F32, name="bbb")
+        for n in range(NB):
+            pb = ps_tr.tile([P, 512], F32, name="pt")
+            nc.tensor.matmul(
+                out=pb[:], lhsT=ones[:], rhs=bbrow[:, n * BLK : (n + 1) * BLK], start=True, stop=True
+            )
+            nc.vector.tensor_copy(out=bbb[:, n * BLK : (n + 1) * BLK], in_=pb[:])
+
+        def copy_on(eng, dst, src):
             if eng == "S":
                 nc.scalar.copy(out=dst, in_=src)
             else:
@@ -108,7 +112,7 @@ def tile_blockdiagmnistconvertible_pa_t_kernel(tc, x, W1, b1, Wb, bb, out):
                             src_words(2 * h + il, u),
                             ident[:],
                         )
-                copy_words(
+                copy_on(
                     engines[h],
                     g32[:, h * 256 : (h + 1) * 256, :],
                     pt[:].rearrange("p (u c) -> p c u", u=2),
@@ -140,21 +144,23 @@ def tile_blockdiagmnistconvertible_pa_t_kernel(tc, x, W1, b1, Wb, bb, out):
 
         def xpath(c):
             x32 = xs[c][:].bitcast(F32)
-            xg = xq.tile([P, 2048], BF16, name="xg", align_bytes=64)
+            xg = xq.tile([P, 2048], BF16, name="xg", align_bytes=64, bufs=3)
             transpose_group(
                 lambda i, u: x32[:, i * 256 + u * P : i * 256 + (u + 1) * P], xg, ("S", "S")
             )
-            xc = xq.tile([P, CW], U32, name="xc", align_bytes=64, bufs=4)
-            xsc = xq.tile([P, CW], U8, name="xsc", align_bytes=64, bufs=4)
+            xc = xq.tile([P, CW], U32, name="xc", align_bytes=64)
+            xsc = xq.tile([P, CW], U8, name="xsc", align_bytes=64)
             quantise(xg, xc, xsc)
             xcs[c] = (xc, xsc)
 
+        hTs = {}
         hcs = {}
 
         def stage1(c):
             xc, xsc = xcs[c]
             for n in range(NB):
                 hT = hp.tile([P, 4 * CW], BF16, name="hT")
+                hTs[(c, n)] = hT
                 for t in range(4):
                     acc = ps_s1.tile([P, CW], F32, name="acc1")
                     nc.tensor.matmul_mx(
@@ -173,28 +179,31 @@ def tile_blockdiagmnistconvertible_pa_t_kernel(tc, x, W1, b1, Wb, bb, out):
                         bias=b1f[:, 4 * n + t : 4 * n + t + 1],
                         scale=1.0,
                     )
+
+        def h_quantise(c):
+            hgs = []
+            for n in range(NB):
                 hg = hp.tile([P, 4 * CW], BF16, name="hg", align_bytes=64)
-                copy_words(
-                    REGROUP[n],
-                    hg[:].rearrange("p (c i t) -> p c t i", i=4, t=4),
-                    hT[:].rearrange("p (t c i) -> p c t i", t=4, i=4),
+                nc.vector.tensor_copy(
+                    out=hg[:].rearrange("p (c i t) -> p c t i", i=4, t=4),
+                    in_=hTs[(c, n)][:].rearrange("p (t c i) -> p c t i", t=4, i=4),
                 )
+                hgs.append(hg)
+            for n in range(NB):
                 hc = hp.tile([P, CW], U32, name="hc%d" % n, align_bytes=64)
                 hsc = hp.tile([P, CW], U8, name="hsc%d" % n, align_bytes=64)
-                quantise(hg, hc, hsc)
+                quantise(hgs[n], hc, hsc)
                 hcs[(c, n)] = (hc, hsc)
 
         def relu2(eng, ap):
             if eng == "V":
                 nc.vector.tensor_scalar_max(out=ap, in0=ap, scalar1=0.0)
-            elif eng == "S":
-                nc.scalar.activation(out=ap, in_=ap, func=ACT.Relu)
             else:
-                nc.gpsimd.tensor_scalar(
-                    out=ap, in0=ap, scalar1=FLT_MAX, scalar2=0.0, op0=ALU.min, op1=ALU.max
-                )
+                nc.scalar.activation(out=ap, in_=ap, func=ACT.Relu)
 
         def stage2(c):
+            engines = relu2_engines(c)
+            rows_per_store = 1 if c == CHUNKS - 1 else 2
             z = zp.tile([P, TILES * HID], F32, name="z")
             for il in range(TILES):
                 for n in range(NB):
@@ -215,9 +224,9 @@ def tile_blockdiagmnistconvertible_pa_t_kernel(tc, x, W1, b1, Wb, bb, out):
                         in1=bbb[:, n * BLK : (n + 1) * BLK],
                         op=ALU.add,
                     )
-                relu2(RELU2[il], z[:, il * HID : (il + 1) * HID])
-                if il % 2 == 1:
-                    lo = (il - 1) * HID
+                relu2(engines[il], z[:, il * HID : (il + 1) * HID])
+                if (il + 1) % rows_per_store == 0:
+                    lo = (il + 1 - rows_per_store) * HID
                     hi = (il + 1) * HID
                     nc.sync.dma_start(
                         out=out_v[:, c * TILES * HID + lo : c * TILES * HID + hi], in_=z[:, lo:hi]
@@ -230,9 +239,11 @@ def tile_blockdiagmnistconvertible_pa_t_kernel(tc, x, W1, b1, Wb, bb, out):
         stage1(0)
         prep_wb(0)
         prep_wb(1)
+        h_quantise(0)
         for c in range(1, CHUNKS):
             if c + 1 < CHUNKS:
                 xpath(c + 1)
             stage1(c)
             stage2(c - 1)
+            h_quantise(c)
         stage2(CHUNKS - 1)

@@ -66,8 +66,8 @@ def tile_blockdiagmnistconvertible_pa_t_kernel(tc, x, W1, b1, Wb, bb, out):
         b1b = const.tile([P, 2 * 4], BF16, name="b1b")
         bbrow = const.tile([P, HID], BF16, name="bbrow")
         ones = const.tile([P, P], BF16, name="ones")
-        nc.vector.memset(bbrow[:], 0.0)
-        nc.vector.memset(ones[:], 1.0)
+        nc.gpsimd.memset(bbrow[:], 0.0)
+        nc.gpsimd.memset(ones[:], 1.0)
         nc.scalar.dma_start(out=bbrow[0:1, :], in_=bb.rearrange("(o n) -> o n", o=1))
         nc.scalar.dma_start(
             out=b1b[:].rearrange("p (n t) -> p n t", t=4),
@@ -88,12 +88,18 @@ def tile_blockdiagmnistconvertible_pa_t_kernel(tc, x, W1, b1, Wb, bb, out):
         nc.vector.tensor_copy(out=b1f[:], in_=b1b[:])
 
         bbb = const.tile([P, HID], F32, name="bbb")
-        for n in range(NB):
-            pb = ps_tr.tile([P, 512], F32, name="pt")
-            nc.tensor.matmul(
-                out=pb[:], lhsT=ones[:], rhs=bbrow[:, n * BLK : (n + 1) * BLK], start=True, stop=True
-            )
-            nc.vector.tensor_copy(out=bbb[:, n * BLK : (n + 1) * BLK], in_=pb[:])
+
+        def spread_bb():
+            for n in range(NB):
+                pb = ps_tr.tile([P, 512], F32, name="pt")
+                nc.tensor.matmul(
+                    out=pb[:],
+                    lhsT=ones[:],
+                    rhs=bbrow[:, n * BLK : (n + 1) * BLK],
+                    start=True,
+                    stop=True,
+                )
+                nc.scalar.copy(out=bbb[:, n * BLK : (n + 1) * BLK], in_=pb[:])
 
         def copy_on(eng, dst, src):
             if eng == "S":
@@ -237,6 +243,7 @@ def tile_blockdiagmnistconvertible_pa_t_kernel(tc, x, W1, b1, Wb, bb, out):
         prep_w1(1)
         xpath(1)
         stage1(0)
+        spread_bb()
         prep_wb(0)
         prep_wb(1)
         h_quantise(0)

@@ -1,6 +1,8 @@
 from contextlib import ExitStack
 
+import concourse.bass as bass
 import concourse.mybir as mybir
+import concourse.tile as tile
 from concourse.masks import make_identity
 
 F32 = mybir.dt.float32
@@ -21,9 +23,8 @@ CW = TILES * P
 
 FLOPS = 2 * B * HID * IN + 2 * B * HID * BLK
 
-
-def relu2_engines(c):
-    return ("S", "S", "S", "V")
+RELU2 = ("S", "V", "S", "V")
+PINNED = False
 
 
 def tile_blockdiagmnistconvertible_pa_t_kernel(tc, x, W1, b1, Wb, bb, out):
@@ -34,17 +35,21 @@ def tile_blockdiagmnistconvertible_pa_t_kernel(tc, x, W1, b1, Wb, bb, out):
         win = ctx.enter_context(tc.tile_pool(name="win", bufs=1))
         wq = ctx.enter_context(tc.tile_pool(name="wq", bufs=1))
         wgp = ctx.enter_context(tc.tile_pool(name="wgp", bufs=2))
-        xq = ctx.enter_context(tc.tile_pool(name="xq", bufs=4))
+        xq = ctx.enter_context(tc.tile_pool(name="xq", bufs=3))
         hp = ctx.enter_context(tc.tile_pool(name="hp", bufs=3))
         zp = ctx.enter_context(tc.tile_pool(name="zp", bufs=3))
         ps_tr = ctx.enter_context(tc.psum_pool(name="ps_tr", bufs=2))
         ps_s1 = ctx.enter_context(tc.psum_pool(name="ps_s1", bufs=3))
         ps_s2 = ctx.enter_context(tc.psum_pool(name="ps_s2", bufs=3))
+        if PINNED:
+            ctx.enter_context(tc.manual_schedule())
 
         x_v = x.rearrange("(p i) k -> p (i k)", i=ROWS_PER_PART)
         out_v = out.rearrange("(p i) o -> p (i o)", i=ROWS_PER_PART)
 
-        xs = [xin.tile([P, TILES * IN], BF16, name="xs%d" % c) for c in range(CHUNKS)]
+        xs = []
+        for c in range(CHUNKS):
+            xs.append(xin.tile([P, TILES * IN], BF16, name="xs%d" % c))
         w1s = [win.tile([P, 4 * IN], BF16, name="w1s%d" % n) for n in range(NB)]
         wbs = [win.tile([P, 4 * BLK], BF16, name="wbs%d" % n) for n in range(NB)]
 
@@ -64,11 +69,7 @@ def tile_blockdiagmnistconvertible_pa_t_kernel(tc, x, W1, b1, Wb, bb, out):
             )
 
         b1b = const.tile([P, 2 * 4], BF16, name="b1b")
-        bbrow = const.tile([P, HID], BF16, name="bbrow")
-        ones = const.tile([P, P], BF16, name="ones")
-        nc.gpsimd.memset(bbrow[:], 0.0)
-        nc.gpsimd.memset(ones[:], 1.0)
-        nc.scalar.dma_start(out=bbrow[0:1, :], in_=bb.rearrange("(o n) -> o n", o=1))
+        bbb = const.tile([P, HID], BF16, name="bbb")
         nc.scalar.dma_start(
             out=b1b[:].rearrange("p (n t) -> p n t", t=4),
             in_=b1.rearrange("(n p t) -> p n t", n=NB, t=4),
@@ -79,6 +80,7 @@ def tile_blockdiagmnistconvertible_pa_t_kernel(tc, x, W1, b1, Wb, bb, out):
         load_x(1)
         load_wb(0)
         load_wb(1)
+        nc.scalar.dma_start(out=bbb[:], in_=bb.partition_broadcast(P))
         for c in range(2, CHUNKS):
             load_x(c)
 
@@ -87,21 +89,7 @@ def tile_blockdiagmnistconvertible_pa_t_kernel(tc, x, W1, b1, Wb, bb, out):
         b1f = const.tile([P, 2 * 4], F32, name="b1f")
         nc.vector.tensor_copy(out=b1f[:], in_=b1b[:])
 
-        bbb = const.tile([P, HID], F32, name="bbb")
-
-        def spread_bb():
-            for n in range(NB):
-                pb = ps_tr.tile([P, 512], F32, name="pt")
-                nc.tensor.matmul(
-                    out=pb[:],
-                    lhsT=ones[:],
-                    rhs=bbrow[:, n * BLK : (n + 1) * BLK],
-                    start=True,
-                    stop=True,
-                )
-                nc.scalar.copy(out=bbb[:, n * BLK : (n + 1) * BLK], in_=pb[:])
-
-        def copy_on(eng, dst, src):
+        def copy_words(eng, dst, src):
             if eng == "S":
                 nc.scalar.copy(out=dst, in_=src)
             else:
@@ -118,7 +106,7 @@ def tile_blockdiagmnistconvertible_pa_t_kernel(tc, x, W1, b1, Wb, bb, out):
                             src_words(2 * h + il, u),
                             ident[:],
                         )
-                copy_on(
+                copy_words(
                     engines[h],
                     g32[:, h * 256 : (h + 1) * 256, :],
                     pt[:].rearrange("p (u c) -> p c u", u=2),
@@ -150,7 +138,7 @@ def tile_blockdiagmnistconvertible_pa_t_kernel(tc, x, W1, b1, Wb, bb, out):
 
         def xpath(c):
             x32 = xs[c][:].bitcast(F32)
-            xg = xq.tile([P, 2048], BF16, name="xg", align_bytes=64, bufs=3)
+            xg = xq.tile([P, 2048], BF16, name="xg", align_bytes=64)
             transpose_group(
                 lambda i, u: x32[:, i * 256 + u * P : i * 256 + (u + 1) * P], xg, ("S", "S")
             )
@@ -159,14 +147,12 @@ def tile_blockdiagmnistconvertible_pa_t_kernel(tc, x, W1, b1, Wb, bb, out):
             quantise(xg, xc, xsc)
             xcs[c] = (xc, xsc)
 
-        hTs = {}
         hcs = {}
 
         def stage1(c):
             xc, xsc = xcs[c]
             for n in range(NB):
                 hT = hp.tile([P, 4 * CW], BF16, name="hT")
-                hTs[(c, n)] = hT
                 for t in range(4):
                     acc = ps_s1.tile([P, CW], F32, name="acc1")
                     nc.tensor.matmul_mx(
@@ -185,31 +171,27 @@ def tile_blockdiagmnistconvertible_pa_t_kernel(tc, x, W1, b1, Wb, bb, out):
                         bias=b1f[:, 4 * n + t : 4 * n + t + 1],
                         scale=1.0,
                     )
-
-        def h_quantise(c):
-            hgs = []
-            for n in range(NB):
                 hg = hp.tile([P, 4 * CW], BF16, name="hg", align_bytes=64)
                 nc.vector.tensor_copy(
                     out=hg[:].rearrange("p (c i t) -> p c t i", i=4, t=4),
-                    in_=hTs[(c, n)][:].rearrange("p (t c i) -> p c t i", t=4, i=4),
+                    in_=hT[:].rearrange("p (t c i) -> p c t i", t=4, i=4),
                 )
-                hgs.append(hg)
-            for n in range(NB):
                 hc = hp.tile([P, CW], U32, name="hc%d" % n, align_bytes=64)
                 hsc = hp.tile([P, CW], U8, name="hsc%d" % n, align_bytes=64)
-                quantise(hgs[n], hc, hsc)
+                quantise(hg, hc, hsc)
                 hcs[(c, n)] = (hc, hsc)
 
         def relu2(eng, ap):
             if eng == "V":
                 nc.vector.tensor_scalar_max(out=ap, in0=ap, scalar1=0.0)
-            else:
+            elif eng == "S":
                 nc.scalar.activation(out=ap, in_=ap, func=ACT.Relu)
+            else:
+                nc.gpsimd.tensor_scalar(
+                    out=ap, in0=ap, scalar1=0.0, scalar2=0.0, op0=ALU.max, op1=ALU.add
+                )
 
         def stage2(c):
-            engines = relu2_engines(c)
-            rows_per_store = 1 if c == CHUNKS - 1 else 2
             z = zp.tile([P, TILES * HID], F32, name="z")
             for il in range(TILES):
                 for n in range(NB):
@@ -230,9 +212,9 @@ def tile_blockdiagmnistconvertible_pa_t_kernel(tc, x, W1, b1, Wb, bb, out):
                         in1=bbb[:, n * BLK : (n + 1) * BLK],
                         op=ALU.add,
                     )
-                relu2(engines[il], z[:, il * HID : (il + 1) * HID])
-                if (il + 1) % rows_per_store == 0:
-                    lo = (il + 1 - rows_per_store) * HID
+                relu2(RELU2[il], z[:, il * HID : (il + 1) * HID])
+                if il % 2 == 1:
+                    lo = (il - 1) * HID
                     hi = (il + 1) * HID
                     nc.sync.dma_start(
                         out=out_v[:, c * TILES * HID + lo : c * TILES * HID + hi], in_=z[:, lo:hi]
@@ -243,14 +225,11 @@ def tile_blockdiagmnistconvertible_pa_t_kernel(tc, x, W1, b1, Wb, bb, out):
         prep_w1(1)
         xpath(1)
         stage1(0)
-        spread_bb()
         prep_wb(0)
         prep_wb(1)
-        h_quantise(0)
         for c in range(1, CHUNKS):
             if c + 1 < CHUNKS:
                 xpath(c + 1)
             stage1(c)
             stage2(c - 1)
-            h_quantise(c)
         stage2(CHUNKS - 1)

@@ -23,7 +23,10 @@ CW = TILES * P
 
 FLOPS = 2 * B * HID * IN + 2 * B * HID * BLK
 
-RELU2 = ("S", "V", "S", "V")
+
+def relu2_engines(c):
+    return ("S", "V", "S", "V") if c == CHUNKS - 1 else (("S", "S", "S", "S") if c >= 4 else ("S", "S", "S", "V"))
+
 PINNED = False
 
 
@@ -35,9 +38,9 @@ def tile_blockdiagmnistconvertible_pa_t_kernel(tc, x, W1, b1, Wb, bb, out):
         win = ctx.enter_context(tc.tile_pool(name="win", bufs=1))
         wq = ctx.enter_context(tc.tile_pool(name="wq", bufs=1))
         wgp = ctx.enter_context(tc.tile_pool(name="wgp", bufs=2))
-        xq = ctx.enter_context(tc.tile_pool(name="xq", bufs=3))
-        hp = ctx.enter_context(tc.tile_pool(name="hp", bufs=3))
-        zp = ctx.enter_context(tc.tile_pool(name="zp", bufs=3))
+        xq = ctx.enter_context(tc.tile_pool(name="xq", bufs=4))
+        hp = ctx.enter_context(tc.tile_pool(name="hp", bufs=4))
+        zp = ctx.enter_context(tc.tile_pool(name="zp", bufs=4))
         ps_tr = ctx.enter_context(tc.psum_pool(name="ps_tr", bufs=2))
         ps_s1 = ctx.enter_context(tc.psum_pool(name="ps_s1", bufs=3))
         ps_s2 = ctx.enter_context(tc.psum_pool(name="ps_s2", bufs=3))
@@ -212,9 +215,10 @@ def tile_blockdiagmnistconvertible_pa_t_kernel(tc, x, W1, b1, Wb, bb, out):
                         in1=bbb[:, n * BLK : (n + 1) * BLK],
                         op=ALU.add,
                     )
-                relu2(RELU2[il], z[:, il * HID : (il + 1) * HID])
-                if il % 2 == 1:
-                    lo = (il - 1) * HID
+                relu2(relu2_engines(c)[il], z[:, il * HID : (il + 1) * HID])
+                rows = 1 if c == CHUNKS - 1 else 2
+                if (il + 1) % rows == 0:
+                    lo = (il + 1 - rows) * HID
                     hi = (il + 1) * HID
                     nc.sync.dma_start(
                         out=out_v[:, c * TILES * HID + lo : c * TILES * HID + hi], in_=z[:, lo:hi]

@@ -72,7 +72,9 @@ def tile_blockdiagmnistconvertible_pa_t_kernel(tc, x, W1, b1, Wb, bb, out):
             )
 
         b1b = const.tile([P, 2 * 4], BF16, name="b1b")
-        bbb = const.tile([P, HID], BF16, name="bbb")
+        bbrow = const.tile([P, HID], BF16, name="bbrow")
+        ones = const.tile([P, P], BF16, name="ones")
+        bbb = const.tile([P, HID], F32, name="bbb")
         nc.scalar.dma_start(
             out=b1b[:].rearrange("p (n t) -> p n t", t=4),
             in_=b1.rearrange("(n p t) -> p n t", n=NB, t=4),
@@ -83,12 +85,26 @@ def tile_blockdiagmnistconvertible_pa_t_kernel(tc, x, W1, b1, Wb, bb, out):
         load_x(1)
         load_wb(0)
         load_wb(1)
-        nc.scalar.dma_start(out=bbb[:], in_=bb.partition_broadcast(P))
         for c in range(2, CHUNKS):
             load_x(c)
 
         ident = const.tile([P, P], F32, name="ident")
         make_identity(nc, ident[:])
+        nc.gpsimd.memset(bbrow[:], 0.0)
+        nc.gpsimd.memset(ones[:], 1.0)
+        nc.scalar.dma_start(out=bbrow[0:1, :], in_=bb.rearrange("(o n) -> o n", o=1))
+
+        def spread_bb():
+            for n in range(NB):
+                pb = ps_tr.tile([P, 512], F32, name="pt")
+                nc.tensor.matmul(
+                    out=pb[:],
+                    lhsT=ones[:],
+                    rhs=bbrow[:, n * BLK : (n + 1) * BLK],
+                    start=True,
+                    stop=True,
+                )
+                nc.scalar.copy(out=bbb[:, n * BLK : (n + 1) * BLK], in_=pb[:])
         b1f = const.tile([P, 2 * 4], F32, name="b1f")
         nc.vector.tensor_copy(out=b1f[:], in_=b1b[:])
 
@@ -151,6 +167,8 @@ def tile_blockdiagmnistconvertible_pa_t_kernel(tc, x, W1, b1, Wb, bb, out):
             xcs[c] = (xc, xsc)
 
         hcs = {}
+        hTs = {}
+        hgs = {}
 
         def stage1(c):
             xc, xsc = xcs[c]
@@ -174,15 +192,27 @@ def tile_blockdiagmnistconvertible_pa_t_kernel(tc, x, W1, b1, Wb, bb, out):
                         bias=b1f[:, 4 * n + t : 4 * n + t + 1],
                         scale=1.0,
                     )
-                hg = hp.tile([P, 4 * CW], BF16, name="hg", align_bytes=64)
-                nc.vector.tensor_copy(
-                    out=hg[:].rearrange("p (c i t) -> p c t i", i=4, t=4),
-                    in_=hT[:].rearrange("p (t c i) -> p c t i", t=4, i=4),
-                )
-                hc = hp.tile([P, CW], U32, name="hc%d" % n, align_bytes=64)
-                hsc = hp.tile([P, CW], U8, name="hsc%d" % n, align_bytes=64)
-                quantise(hg, hc, hsc)
-                hcs[(c, n)] = (hc, hsc)
+                hTs[(c, n)] = hT
+
+        def regroup(c, n):
+            hg = hp.tile([P, 4 * CW], BF16, name="hg", align_bytes=64)
+            nc.vector.tensor_copy(
+                out=hg[:].rearrange("p (c i t) -> p c t i", i=4, t=4),
+                in_=hTs[(c, n)][:].rearrange("p (t c i) -> p c t i", t=4, i=4),
+            )
+            hgs[(c, n)] = hg
+
+        def h_quantise(c, n):
+            hc = hp.tile([P, CW], U32, name="hc%d" % n, align_bytes=64)
+            hsc = hp.tile([P, CW], U8, name="hsc%d" % n, align_bytes=64)
+            quantise(hgs[(c, n)], hc, hsc)
+            hcs[(c, n)] = (hc, hsc)
+
+        def next_h_step(c, step):
+            if step < 2:
+                regroup(c, step)
+            else:
+                h_quantise(c, step - 2)
 
         def relu2(eng, ap):
             if eng == "V":
@@ -216,6 +246,8 @@ def tile_blockdiagmnistconvertible_pa_t_kernel(tc, x, W1, b1, Wb, bb, out):
                         op=ALU.add,
                     )
                 relu2(relu2_engines(c)[il], z[:, il * HID : (il + 1) * HID])
+                if c + 1 < CHUNKS:
+                    next_h_step(c + 1, il)
                 rows = 1 if c == CHUNKS - 1 else 2
                 if (il + 1) % rows == 0:
                     lo = (il + 1 - rows) * HID
@@ -229,8 +261,11 @@ def tile_blockdiagmnistconvertible_pa_t_kernel(tc, x, W1, b1, Wb, bb, out):
         prep_w1(1)
         xpath(1)
         stage1(0)
+        spread_bb()
         prep_wb(0)
         prep_wb(1)
+        for step in range(4):
+            next_h_step(0, step)
         for c in range(1, CHUNKS):
             if c + 1 < CHUNKS:
                 xpath(c + 1)

from contextlib import ExitStack

import concourse.bass as bass
import concourse.mybir as mybir
import concourse.tile as tile
from concourse.masks import make_identity

F32 = mybir.dt.float32
BF16 = mybir.dt.bfloat16
U32 = mybir.dt.uint32
U8 = mybir.dt.uint8
FP8X4 = mybir.dt.float8_e4m3fn_x4
ALU = mybir.AluOpType
ACT = mybir.ActivationFunctionType

P = 128
B, IN, HID, BLK = 4096, 512, 1024, 512
NB = HID // BLK
ROWS_PER_PART = B // P
TILES = 4
CHUNKS = ROWS_PER_PART // TILES
CW = TILES * P

FLOPS = 2 * B * HID * IN + 2 * B * HID * BLK


def relu2_engines(c):
    return ("S", "V", "S", "V") if c == CHUNKS - 1 else (("S", "S", "S", "S") if c >= 4 else ("S", "S", "S", "V"))

PINNED = False


def tile_blockdiagmnistconvertible_pa_t_kernel(tc, x, W1, b1, Wb, bb, out):
    nc = tc.nc
    with ExitStack() as ctx:
        const = ctx.enter_context(tc.tile_pool(name="const", bufs=1))
        xin = ctx.enter_context(tc.tile_pool(name="xin", bufs=1))
        win = ctx.enter_context(tc.tile_pool(name="win", bufs=1))
        wq = ctx.enter_context(tc.tile_pool(name="wq", bufs=1))
        wgp = ctx.enter_context(tc.tile_pool(name="wgp", bufs=2))
        xq = ctx.enter_context(tc.tile_pool(name="xq", bufs=4))
        hp = ctx.enter_context(tc.tile_pool(name="hp", bufs=4))
        zp = ctx.enter_context(tc.tile_pool(name="zp", bufs=4))
        ps_tr = ctx.enter_context(tc.psum_pool(name="ps_tr", bufs=2))
        ps_s1 = ctx.enter_context(tc.psum_pool(name="ps_s1", bufs=3))
        ps_s2 = ctx.enter_context(tc.psum_pool(name="ps_s2", bufs=3))
        if PINNED:
            ctx.enter_context(tc.manual_schedule())

        x_v = x.rearrange("(p i) k -> p (i k)", i=ROWS_PER_PART)
        out_v = out.rearrange("(p i) o -> p (i o)", i=ROWS_PER_PART)

        xs = []
        for c in range(CHUNKS):
            xs.append(xin.tile([P, TILES * IN], BF16, name="xs%d" % c))
        w1s = [win.tile([P, 4 * IN], BF16, name="w1s%d" % n) for n in range(NB)]
        wbs = [win.tile([P, 4 * BLK], BF16, name="wbs%d" % n) for n in range(NB)]

        def load_x(c):
            nc.sync.dma_start(out=xs[c][:], in_=x_v[:, c * TILES * IN : (c + 1) * TILES * IN])

        def load_w1(n):
            nc.sync.dma_start(
                out=w1s[n][:],
                in_=W1[n * BLK : (n + 1) * BLK, :].rearrange("(p t) k -> p (t k)", t=4),
            )

        def load_wb(n):
            nc.sync.dma_start(
                out=wbs[n][:].rearrange("p (j k) -> p j k", j=4),
                in_=Wb[n].rearrange("(j p) k -> p j k", p=P),
            )

        b1b = const.tile([P, 2 * 4], BF16, name="b1b")
        bbrow = const.tile([P, HID], BF16, name="bbrow")
        ones = const.tile([P, P], BF16, name="ones")
        bbb = const.tile([P, HID], F32, name="bbb")
        nc.scalar.dma_start(
            out=b1b[:].rearrange("p (n t) -> p n t", t=4),
            in_=b1.rearrange("(n p t) -> p n t", n=NB, t=4),
        )
        load_x(0)
        load_w1(0)
        load_w1(1)
        load_x(1)
        load_wb(0)
        load_wb(1)
        for c in range(2, CHUNKS):
            load_x(c)

        ident = const.tile([P, P], F32, name="ident")
        make_identity(nc, ident[:])
        nc.gpsimd.memset(bbrow[:], 0.0)
        nc.gpsimd.memset(ones[:], 1.0)
        nc.scalar.dma_start(out=bbrow[0:1, :], in_=bb.rearrange("(o n) -> o n", o=1))

        def spread_bb():
            for n in range(NB):
                pb = ps_tr.tile([P, 512], F32, name="pt")
                nc.tensor.matmul(
                    out=pb[:],
                    lhsT=ones[:],
                    rhs=bbrow[:, n * BLK : (n + 1) * BLK],
                    start=True,
                    stop=True,
                )
                nc.scalar.copy(out=bbb[:, n * BLK : (n + 1) * BLK], in_=pb[:])
        b1f = const.tile([P, 2 * 4], F32, name="b1f")
        nc.vector.tensor_copy(out=b1f[:], in_=b1b[:])

        def copy_words(eng, dst, src):
            if eng == "S":
                nc.scalar.copy(out=dst, in_=src)
            else:
                nc.vector.tensor_copy(out=dst, in_=src)

        def transpose_group(src_words, grouped, engines):
            g32 = grouped[:].bitcast(F32).rearrange("p (c u) -> p c u", u=2)
            for h in range(2):
                pt = ps_tr.tile([P, 512], F32, name="pt")
                for il in range(2):
                    for u in range(2):
                        nc.tensor.transpose(
                            pt[:, u * 256 + il * P : u * 256 + (il + 1) * P],
                            src_words(2 * h + il, u),
                            ident[:],
                        )
                copy_words(
                    engines[h],
                    g32[:, h * 256 : (h + 1) * 256, :],
                    pt[:].rearrange("p (u c) -> p c u", u=2),
                )

        def quantise(grouped, codes, scales):
            nc.vector.quantize_mx(out=codes[:].bitcast(FP8X4), scales=scales[:], in_=grouped[:])

        w1c = [wq.tile([P, 512], U32, name="w1c%d" % n, align_bytes=64) for n in range(NB)]
        w1sc = [wq.tile([P, 512], U8, name="w1sc%d" % n, align_bytes=64) for n in range(NB)]
        wbc = [wq.tile([P, 512], U32, name="wbc%d" % n, align_bytes=64) for n in range(NB)]
        wbsc = [wq.tile([P, 512], U8, name="wbsc%d" % n, align_bytes=64) for n in range(NB)]

        def prep_w1(n):
            w32 = w1s[n][:].bitcast(F32)
            wg = wgp.tile([P, 2048], BF16, name="wg", align_bytes=64)
            transpose_group(
                lambda t, u: w32[:, t * 256 + u * P : t * 256 + (u + 1) * P], wg, ("V", "S")
            )
            quantise(wg, w1c[n], w1sc[n])

        def prep_wb(n):
            w32 = wbs[n][:].bitcast(F32).rearrange("p (j q u) -> p j q u", j=4, u=2)
            wg = wgp.tile([P, 2048], BF16, name="wg", align_bytes=64)
            transpose_group(lambda j, u: w32[:, j, :, u], wg, ("V", "S"))
            quantise(wg, wbc[n], wbsc[n])

        xcs = {}

        def xpath(c):
            x32 = xs[c][:].bitcast(F32)
            xg = xq.tile([P, 2048], BF16, name="xg", align_bytes=64)
            transpose_group(
                lambda i, u: x32[:, i * 256 + u * P : i * 256 + (u + 1) * P], xg, ("S", "S")
            )
            xc = xq.tile([P, CW], U32, name="xc", align_bytes=64)
            xsc = xq.tile([P, CW], U8, name="xsc", align_bytes=64)
            quantise(xg, xc, xsc)
            xcs[c] = (xc, xsc)

        hcs = {}
        hTs = {}
        hgs = {}

        def stage1(c):
            xc, xsc = xcs[c]
            for n in range(NB):
                hT = hp.tile([P, 4 * CW], BF16, name="hT")
                for t in range(4):
                    acc = ps_s1.tile([P, CW], F32, name="acc1")
                    nc.tensor.matmul_mx(
                        out=acc[:],
                        lhsT=w1c[n][:, t * P : (t + 1) * P].bitcast(FP8X4),
                        lhsT_scale=w1sc[n][:, t * P : (t + 1) * P],
                        rhs=xc[:].bitcast(FP8X4),
                        rhs_scale=xsc[:],
                        start=True,
                        stop=True,
                    )
                    nc.scalar.activation(
                        out=hT[:, t * CW : (t + 1) * CW],
                        in_=acc[:],
                        func=ACT.Relu,
                        bias=b1f[:, 4 * n + t : 4 * n + t + 1],
                        scale=1.0,
                    )
                hTs[(c, n)] = hT

        def regroup(c, n):
            hg = hp.tile([P, 4 * CW], BF16, name="hg", align_bytes=64)
            nc.vector.tensor_copy(
                out=hg[:].rearrange("p (c i t) -> p c t i", i=4, t=4),
                in_=hTs[(c, n)][:].rearrange("p (t c i) -> p c t i", t=4, i=4),
            )
            hgs[(c, n)] = hg

        def h_quantise(c, n):
            hc = hp.tile([P, CW], U32, name="hc%d" % n, align_bytes=64)
            hsc = hp.tile([P, CW], U8, name="hsc%d" % n, align_bytes=64)
            quantise(hgs[(c, n)], hc, hsc)
            hcs[(c, n)] = (hc, hsc)

        def next_h_step(c, step):
            if step < 2:
                regroup(c, step)
            else:
                h_quantise(c, step - 2)

        def relu2(eng, ap):
            if eng == "V":
                nc.vector.tensor_scalar_max(out=ap, in0=ap, scalar1=0.0)
            elif eng == "S":
                nc.scalar.activation(out=ap, in_=ap, func=ACT.Relu)
            else:
                nc.gpsimd.tensor_scalar(
                    out=ap, in0=ap, scalar1=0.0, scalar2=0.0, op0=ALU.max, op1=ALU.add
                )

        def stage2(c):
            z = zp.tile([P, TILES * HID], F32, name="z")
            for il in range(TILES):
                for n in range(NB):
                    hc, hsc = hcs[(c, n)]
                    acc = ps_s2.tile([P, BLK], F32, name="acc2")
                    nc.tensor.matmul_mx(
                        out=acc[:],
                        lhsT=hc[:, il * P : (il + 1) * P].bitcast(FP8X4),
                        lhsT_scale=hsc[:, il * P : (il + 1) * P],
                        rhs=wbc[n][:].bitcast(FP8X4),
                        rhs_scale=wbsc[n][:],
                        start=True,
                        stop=True,
                    )
                    nc.vector.tensor_tensor(
                        out=z[:, il * HID + n * BLK : il * HID + (n + 1) * BLK],
                        in0=acc[:],
                        in1=bbb[:, n * BLK : (n + 1) * BLK],
                        op=ALU.add,
                    )
                relu2(relu2_engines(c)[il], z[:, il * HID : (il + 1) * HID])
                if c + 1 < CHUNKS:
                    next_h_step(c + 1, il)
                rows = 1 if c == CHUNKS - 1 else 2
                if (il + 1) % rows == 0:
                    lo = (il + 1 - rows) * HID
                    hi = (il + 1) * HID
                    nc.sync.dma_start(
                        out=out_v[:, c * TILES * HID + lo : c * TILES * HID + hi], in_=z[:, lo:hi]
                    )

        xpath(0)
        prep_w1(0)
        prep_w1(1)
        xpath(1)
        stage1(0)
        spread_bb()
        prep_wb(0)
        prep_wb(1)
        for step in range(4):
            next_h_step(0, step)
        for c in range(1, CHUNKS):
            if c + 1 < CHUNKS:
                xpath(c + 1)
            stage1(c)
            stage2(c - 1)
        stage2(CHUNKS - 1)
